import numpy as np
import ml_dtypes


def mxq(x, axis, fmt="e4m3"):
    dtype, down = {"e4m3": (ml_dtypes.float8_e4m3fn, 7), "e5m2": (ml_dtypes.float8_e5m2, 14)}[fmt]
    v = np.moveaxis(np.asarray(x, np.float32).astype(ml_dtypes.bfloat16).astype(np.float64), axis, -1)
    blocks = v.reshape(v.shape[:-1] + (-1, 32))
    amax = np.abs(blocks).max(-1, keepdims=True)
    byte = np.maximum(np.where(amax > 0, np.frexp(amax)[1] - 1 + 127, 0) - down, 1)
    scale = np.exp2(byte - 127.0)
    codes = (blocks / scale).astype(np.float32).astype(dtype).astype(np.float64)
    return np.moveaxis((codes * scale).reshape(v.shape), -1, axis)


WIDE = False


def mx_kscale(k):
    if not WIDE:
        return np.ones(k)
    levels = np.array([10, -10, 5, -5, 0])
    a = np.random.permutation(np.resize(levels, k // 512 * 4)).reshape(k // 512, 4)
    idx = np.arange(k)
    return np.exp2(a[idx // 512, idx % 128 // 32])


BF16 = ml_dtypes.bfloat16


def bf(x):
    return np.asarray(x, np.float32).astype(BF16)


def f64(x):
    return np.asarray(x).astype(np.float64)


B, S, D, H, HD, M, G = 4, 128, 1024, 8, 128, 4096, 3
EPS = 1e-6
HH = H * HD


def silu(v):
    return v / (1.0 + np.exp(-v))


def rmsnorm(x, gain):
    var = np.mean(np.square(x), axis=-1, keepdims=True)
    return x * (1.0 / np.sqrt(var + EPS)) * gain


def setup_inputs():
    s, t = mx_kscale(HH), mx_kscale(D)
    return {"attn": bf(0.3 * np.random.standard_normal((B, S, HH)) * s),
            "x": bf(np.random.standard_normal((B, S, D))),
            "w_o": bf(np.random.standard_normal((HH, D)) * 2.0 / np.sqrt(HH) / s[:, None]),
            "rms2_scale": bf((1.0 + 0.1 * np.random.standard_normal(D)) * t),
            "w_gate": bf(np.random.standard_normal((D, M)) / np.sqrt(D) / t[:, None]),
            "w_up": bf(np.random.standard_normal((D, M)) / np.sqrt(D) / t[:, None])}


def reference(attn, x, w_o, rms2_scale, w_gate, w_up):
    x_mid = f64(x) + (mxq(f64(attn), 2, "e4m3") @ mxq(f64(w_o), 0, "e4m3"))
    hq = mxq(rmsnorm(x_mid, f64(rms2_scale)), 2, "e4m3")
    g = silu(hq @ mxq(f64(w_gate), 0, "e4m3")) * (hq @ mxq(f64(w_up), 0, "e4m3"))
    return x_mid, g

@@ -1,0 +1,249 @@
+from contextlib import ExitStack
+
+import concourse.mybir as mybir
+from concourse.masks import make_identity
+
+F32 = mybir.dt.float32
+BF16 = mybir.dt.bfloat16
+U32 = mybir.dt.uint32
+U8 = mybir.dt.uint8
+FP8X4 = mybir.dt.float8_e4m3fn_x4
+ACT = mybir.ActivationFunctionType
+ALU = mybir.AluOpType
+
+P = 128
+PACK = 4
+K_PASS = P * PACK
+TOKENS = 512
+D_MODEL = 1024
+D_FF = 4096
+TOKEN_TILES = TOKENS // P
+PASSES = D_MODEL // K_PASS
+N_TILE = 512
+LOAD_COLS = 1024
+RUN = 4
+EPS = 1e-6
+
+FLOPS = 2 * TOKENS * D_MODEL * (D_MODEL + 2 * D_FF)
+
+
+def quantise_weight_cols(nc, stage, raw_cols, codes, scales, copy):
+    grouped = stage.tile([P, N_TILE, PACK], BF16, align_bytes=64)
+    copy(
+        out=grouped[:].rearrange("p (c i) t -> p c t i", i=RUN),
+        in_=raw_cols.rearrange("p t (c i) -> p c t i", i=RUN),
+    )
+    nc.vector.quantize_mx(
+        out=codes.bitcast(FP8X4),
+        scales=scales,
+        in_=grouped[:].rearrange("p n t -> p (n t)"),
+    )
+
+
+def tile_transformerblocktpu_pb_kernel(
+    tc, attn, x, w_o, rms2_scale, w_gate, w_up, out_0, out_1
+):
+    nc = tc.nc
+    attn_rows = attn.flatten_outer_dims()
+    x_rows = x.flatten_outer_dims()
+    xmid_rows = out_0.flatten_outer_dims()
+    g_rows = out_1.flatten_outer_dims()
+
+    with ExitStack() as ctx:
+        consts = ctx.enter_context(tc.tile_pool(name="consts", bufs=1))
+        keep = ctx.enter_context(tc.tile_pool(name="keep", bufs=1))
+        raw_pool = ctx.enter_context(tc.tile_pool(name="raw", bufs=9))
+        stage = ctx.enter_context(tc.tile_pool(name="stage", bufs=6))
+        rows = ctx.enter_context(tc.tile_pool(name="rows", bufs=2))
+        codes_pool = ctx.enter_context(tc.tile_pool(name="codes", bufs=4))
+        ep = ctx.enter_context(tc.tile_pool(name="ep", bufs=3))
+        out_pool = ctx.enter_context(tc.tile_pool(name="out", bufs=6))
+        acc = ctx.enter_context(tc.psum_pool(name="acc", bufs=6))
+        tp = ctx.enter_context(tc.psum_pool(name="tp", bufs=2))
+
+        eps = consts.tile([P, 1], F32)
+        nc.vector.memset(eps[:], EPS)
+        warm = consts.tile([P, 1], F32)
+        nc.scalar.activation(out=warm[:], in_=eps[:], func=ACT.Sqrt)
+        ident_f32 = consts.tile([P, P], F32)
+        make_identity(nc, ident_f32[:])
+        ident_bf16 = consts.tile([P, P], BF16)
+        make_identity(nc, ident_bf16[:])
+
+        gain_row = consts.tile([P, D_MODEL], BF16)
+        nc.vector.memset(gain_row[:], 0.0)
+        nc.sync.dma_start(out=gain_row[0:1, :], in_=rms2_scale.unsqueeze(0))
+        attn_sb = keep.tile([P, TOKEN_TILES, D_MODEL], BF16)
+        for i in range(TOKEN_TILES):
+            nc.sync.dma_start(out=attn_sb[:, i, :], in_=attn_rows[i * P : (i + 1) * P, :])
+        wo_raw = []
+        for g in range(PASSES):
+            raw = raw_pool.tile([P, PACK, LOAD_COLS], BF16, tag="raw")
+            nc.sync.dma_start(
+                out=raw[:].rearrange("q (u e) n -> q u e n", e=2),
+                in_=w_o[g * K_PASS : (g + 1) * K_PASS, :].rearrange(
+                    "(u q e) n -> q u e n", u=2, e=2
+                ),
+            )
+            wo_raw.append(raw)
+        x_sb = keep.tile([P, TOKEN_TILES, D_MODEL], BF16)
+        nc.sync.dma_start(out=x_sb[:], in_=x_rows.rearrange("(i p) d -> p i d", p=P))
+
+        a_grouped = keep.tile([P, TOKEN_TILES, PASSES, P, PACK], BF16, align_bytes=64)
+        a_codes = keep.tile([P, TOKEN_TILES, PASSES, P], U32, align_bytes=64)
+        a_scales = keep.tile([P, TOKEN_TILES, PASSES, P], U8, align_bytes=64)
+        for i in range(TOKEN_TILES):
+            attn_words = attn_sb[:, i, :].bitcast(F32)
+            at = tp.tile([P, PASSES, 2, P], F32, tag="tp")
+            for g in range(PASSES):
+                for u in range(2):
+                    first = (2 * g + u) * P
+                    nc.tensor.transpose(
+                        out=at[:, g, u, :],
+                        in_=attn_words[:, first : first + P],
+                        identity=ident_f32[:],
+                    )
+            nc.scalar.copy(
+                out=a_grouped[:, i].bitcast(F32),
+                in_=at[:].rearrange("q g u r -> q g r u"),
+            )
+        nc.vector.quantize_mx(
+            out=a_codes[:].rearrange("q i g r -> q (i g r)").bitcast(FP8X4),
+            scales=a_scales[:].rearrange("q i g r -> q (i g r)"),
+            in_=a_grouped[:].rearrange("q i g r t -> q (i g r t)"),
+        )
+
+        wo_codes = keep.tile([P, PASSES, D_MODEL], U32, align_bytes=64)
+        wo_scales = keep.tile([P, PASSES, D_MODEL], U8, align_bytes=64)
+        for g in range(PASSES):
+            for half in range(D_MODEL // N_TILE):
+                cols = slice(half * N_TILE, (half + 1) * N_TILE)
+                quantise_weight_cols(
+                    nc,
+                    stage,
+                    wo_raw[g][:, :, cols],
+                    wo_codes[:, g, cols],
+                    wo_scales[:, g, cols],
+                    nc.vector.tensor_copy if (g + half) % 2 == 0 else nc.scalar.copy,
+                )
+
+        ones = consts.tile([P, P], BF16)
+        nc.vector.memset(ones[:], 1.0)
+        gain_all = consts.tile([P, D_MODEL], BF16)
+        for half in range(D_MODEL // N_TILE):
+            cols = slice(half * N_TILE, (half + 1) * N_TILE)
+            gain_ps = acc.tile([P, N_TILE], F32, tag="acc")
+            nc.tensor.matmul(
+                out=gain_ps[:], lhsT=ones[:], rhs=gain_row[:, cols], start=True, stop=True
+            )
+            nc.scalar.copy(out=gain_all[:, cols], in_=gain_ps[:])
+
+        xmid = keep.tile([P, TOKEN_TILES, D_MODEL], F32)
+        sumsq = keep.tile([P, TOKEN_TILES], F32)
+        for i in range(TOKEN_TILES):
+            for half in range(D_MODEL // N_TILE):
+                cols = slice(half * N_TILE, (half + 1) * N_TILE)
+                xm_ps = acc.tile([P, N_TILE], F32, tag="acc")
+                for g in range(PASSES):
+                    nc.tensor.matmul_mx(
+                        out=xm_ps[:],
+                        lhsT=a_codes[:, i, g, :].bitcast(FP8X4),
+                        lhsT_scale=a_scales[:, i, g, :],
+                        rhs=wo_codes[:, g, cols].bitcast(FP8X4),
+                        rhs_scale=wo_scales[:, g, cols],
+                        start=(g == 0),
+                        stop=(g == PASSES - 1),
+                    )
+                nc.vector.tensor_tensor(
+                    out=xmid[:, i, cols], in0=xm_ps[:], in1=x_sb[:, i, cols], op=ALU.add
+                )
+            nc.gpsimd.dma_start(out=xmid_rows[i * P : (i + 1) * P, :], in_=xmid[:, i, :])
+            squares = rows.tile([P, D_MODEL], BF16)
+            nc.scalar.activation(
+                out=squares[:], in_=xmid[:, i, :], func=ACT.Square, accum_out=sumsq[:, i : i + 1]
+            )
+
+        rms = keep.tile([P, TOKEN_TILES], F32)
+        nc.scalar.activation(
+            out=rms[:], in_=sumsq[:], func=ACT.Sqrt, scale=1.0 / D_MODEL, bias=eps[:, 0:1]
+        )
+        inv_rms = keep.tile([P, TOKEN_TILES], F32)
+        nc.vector.reciprocal(out=inv_rms[:], in_=rms[:])
+
+        h_codes = keep.tile([P, TOKEN_TILES, PASSES, P], U32, align_bytes=64)
+        h_scales = keep.tile([P, TOKEN_TILES, PASSES, P], U8, align_bytes=64)
+        for i in range(TOKEN_TILES):
+            h_bf16 = rows.tile([P, D_MODEL], BF16)
+            nc.vector.scalar_tensor_tensor(
+                out=h_bf16[:],
+                in0=xmid[:, i, :],
+                scalar=inv_rms[:, i : i + 1],
+                in1=gain_all[:],
+                op0=ALU.mult,
+                op1=ALU.mult,
+            )
+            ht = tp.tile([P, PASSES * PACK, P], BF16, tag="tp")
+            for j in range(PASSES * PACK):
+                nc.tensor.transpose(
+                    out=ht[:, j, :], in_=h_bf16[:, j * P : (j + 1) * P], identity=ident_bf16[:]
+                )
+            h_grouped = rows.tile([P, PASSES, P, PACK], BF16, align_bytes=64)
+            nc.scalar.copy(
+                out=h_grouped[:], in_=ht[:].rearrange("p (g t) r -> p g r t", t=PACK)
+            )
+            nc.vector.quantize_mx(
+                out=h_codes[:, i].rearrange("p g r -> p (g r)").bitcast(FP8X4),
+                scales=h_scales[:, i].rearrange("p g r -> p (g r)"),
+                in_=h_grouped[:].rearrange("p g r t -> p (g r t)"),
+            )
+
+        for pair in range(D_FF // LOAD_COLS):
+            raws = []
+            for w in (w_gate, w_up):
+                for g in range(PASSES):
+                    raw = raw_pool.tile([P, PACK, LOAD_COLS], BF16, tag="raw")
+                    nc.sync.dma_start(
+                        out=raw[:],
+                        in_=w[
+                            g * K_PASS : (g + 1) * K_PASS,
+                            pair * LOAD_COLS : (pair + 1) * LOAD_COLS,
+                        ].rearrange("(t p) n -> p t n", p=P),
+                    )
+                    raws.append(raw)
+            for half in range(LOAD_COLS // N_TILE):
+                cols = slice(half * N_TILE, (half + 1) * N_TILE)
+                first_col = pair * LOAD_COLS + half * N_TILE
+                w_codes = codes_pool.tile([P, 2, PASSES, N_TILE], U32, align_bytes=64)
+                w_scales = codes_pool.tile([P, 2, PASSES, N_TILE], U8, align_bytes=64)
+                for m in range(2):
+                    for g in range(PASSES):
+                        quantise_weight_cols(
+                            nc,
+                            stage,
+                            raws[m * PASSES + g][:, :, cols],
+                            w_codes[:, m, g, :],
+                            w_scales[:, m, g, :],
+                            nc.vector.tensor_copy if (g + m) % 2 == 0 else nc.scalar.copy,
+                        )
+                for i in range(TOKEN_TILES):
+                    gate_ps = acc.tile([P, N_TILE], F32, tag="acc")
+                    up_ps = acc.tile([P, N_TILE], F32, tag="acc")
+                    for m, product in enumerate((gate_ps, up_ps)):
+                        for g in range(PASSES):
+                            nc.tensor.matmul_mx(
+                                out=product[:],
+                                lhsT=h_codes[:, i, g, :].bitcast(FP8X4),
+                                lhsT_scale=h_scales[:, i, g, :],
+                                rhs=w_codes[:, m, g, :].bitcast(FP8X4),
+                                rhs_scale=w_scales[:, m, g, :],
+                                start=(g == 0),
+                                stop=(g == PASSES - 1),
+                            )
+                    silu = ep.tile([P, N_TILE], F32)
+                    nc.scalar.activation(out=silu[:], in_=gate_ps[:], func=ACT.Silu)
+                    g_sb = out_pool.tile([P, N_TILE], F32)
+                    nc.vector.tensor_tensor(out=g_sb[:], in0=up_ps[:], in1=silu[:], op=ALU.mult)
+                    nc.gpsimd.dma_start(
+                        out=g_rows[i * P : (i + 1) * P, first_col : first_col + N_TILE],
+                        in_=g_sb[:],
+                    )

@@ -20,23 +20,21 @@ D_FF = 4096
 TOKEN_TILES = TOKENS // P
 PASSES = D_MODEL // K_PASS
 N_TILE = 512
-LOAD_COLS = 1024
+CHUNKS = D_FF // N_TILE
+LOAD_COLS = 2 * N_TILE
+PAIRS = D_FF // LOAD_COLS
+PIECE = N_TILE // 2
 RUN = 4
+GATE, UP = 0, 1
 EPS = 1e-6
 
 FLOPS = 2 * TOKENS * D_MODEL * (D_MODEL + 2 * D_FF)
 
 
-def quantise_weight_cols(nc, stage, raw_cols, codes, scales, copy):
-    grouped = stage.tile([P, N_TILE, PACK], BF16, align_bytes=64)
+def regroup(copy, grouped_cols, raw_cols):
     copy(
-        out=grouped[:].rearrange("p (c i) t -> p c t i", i=RUN),
+        out=grouped_cols.rearrange("p (c i) t -> p c t i", i=RUN),
         in_=raw_cols.rearrange("p t (c i) -> p c t i", i=RUN),
-    )
-    nc.vector.quantize_mx(
-        out=codes.bitcast(FP8X4),
-        scales=scales,
-        in_=grouped[:].rearrange("p n t -> p (n t)"),
     )
 
 
@@ -53,29 +51,83 @@ def tile_transformerblocktpu_pb_kernel(
         consts = ctx.enter_context(tc.tile_pool(name="consts", bufs=1))
         keep = ctx.enter_context(tc.tile_pool(name="keep", bufs=1))
         raw_pool = ctx.enter_context(tc.tile_pool(name="raw", bufs=9))
-        stage = ctx.enter_context(tc.tile_pool(name="stage", bufs=6))
+        stage = ctx.enter_context(tc.tile_pool(name="stage", bufs=3))
         rows = ctx.enter_context(tc.tile_pool(name="rows", bufs=2))
-        codes_pool = ctx.enter_context(tc.tile_pool(name="codes", bufs=4))
+        codes_pool = ctx.enter_context(tc.tile_pool(name="codes", bufs=3))
         ep = ctx.enter_context(tc.tile_pool(name="ep", bufs=3))
-        out_pool = ctx.enter_context(tc.tile_pool(name="out", bufs=6))
+        out_pool = ctx.enter_context(tc.tile_pool(name="out", bufs=8))
         acc = ctx.enter_context(tc.psum_pool(name="acc", bufs=6))
         tp = ctx.enter_context(tc.psum_pool(name="tp", bufs=2))
+        ctx.enter_context(tc.manual_schedule())
+
+        raws = {}
+        grouped = {}
+        w_codes = {}
+        w_scales = {}
+
+        def load_pair(pair):
+            for m, w in enumerate((w_gate, w_up)):
+                for g in range(PASSES):
+                    raw = raw_pool.tile([P, PACK, LOAD_COLS], BF16, tag="raw")
+                    nc.sync.dma_start(
+                        out=raw[:],
+                        in_=w[
+                            g * K_PASS : (g + 1) * K_PASS,
+                            pair * LOAD_COLS : (pair + 1) * LOAD_COLS,
+                        ].rearrange("(t p) n -> p t n", p=P),
+                    )
+                    raws[(pair, m, g)] = raw
+
+        def raw_cols(chunk, m, g, first, width):
+            start = (chunk % 2) * N_TILE + first
+            return raws[(chunk // 2, m, g)][:, :, start : start + width]
+
+        def vector_regroup(chunk, m):
+            if chunk < CHUNKS:
+                by_vector = stage.tile([P, N_TILE, PACK], BF16, align_bytes=64)
+                regroup(nc.vector.tensor_copy, by_vector[:], raw_cols(chunk, m, 0, 0, N_TILE))
+                grouped[(chunk, m, 0)] = by_vector
+
+        def scalar_regroup(chunk, piece):
+            if chunk < CHUNKS:
+                m, part = divmod(piece, 2)
+                if part == 0:
+                    by_scalar = stage.tile([P, N_TILE, PACK], BF16, align_bytes=64)
+                    grouped[(chunk, m, 1)] = by_scalar
+                first = part * PIECE
+                regroup(
+                    nc.scalar.copy,
+                    grouped[(chunk, m, 1)][:, first : first + PIECE, :],
+                    raw_cols(chunk, m, 1, first, PIECE),
+                )
+
+        def quantise(chunk, m, g):
+            if chunk < CHUNKS:
+                if chunk not in w_codes:
+                    codes = codes_pool.tile([P, 2, PASSES, N_TILE], U32, align_bytes=64)
+                    scales = codes_pool.tile([P, 2, PASSES, N_TILE], U8, align_bytes=64)
+                    w_codes[chunk] = codes
+                    w_scales[chunk] = scales
+                nc.vector.quantize_mx(
+                    out=w_codes[chunk][:, m, g, :].bitcast(FP8X4),
+                    scales=w_scales[chunk][:, m, g, :],
+                    in_=grouped[(chunk, m, g)][:].rearrange("p n t -> p (n t)"),
+                )
 
         eps = consts.tile([P, 1], F32)
         nc.vector.memset(eps[:], EPS)
-        warm = consts.tile([P, 1], F32)
-        nc.scalar.activation(out=warm[:], in_=eps[:], func=ACT.Sqrt)
+        gain_row = consts.tile([P, D_MODEL], BF16)
+        nc.vector.memset(gain_row[:], 0.0)
+        ones = consts.tile([P, P], BF16)
+        nc.vector.memset(ones[:], 1.0)
+        warm = consts.tile([P, 2], F32)
+        nc.scalar.activation(out=warm[:, 0:1], in_=eps[:], func=ACT.Sqrt)
         ident_f32 = consts.tile([P, P], F32)
         make_identity(nc, ident_f32[:])
         ident_bf16 = consts.tile([P, P], BF16)
         make_identity(nc, ident_bf16[:])
 
-        gain_row = consts.tile([P, D_MODEL], BF16)
-        nc.vector.memset(gain_row[:], 0.0)
         nc.sync.dma_start(out=gain_row[0:1, :], in_=rms2_scale.unsqueeze(0))
-        attn_sb = keep.tile([P, TOKEN_TILES, D_MODEL], BF16)
-        for i in range(TOKEN_TILES):
-            nc.sync.dma_start(out=attn_sb[:, i, :], in_=attn_rows[i * P : (i + 1) * P, :])
         wo_raw = []
         for g in range(PASSES):
             raw = raw_pool.tile([P, PACK, LOAD_COLS], BF16, tag="raw")
@@ -86,8 +138,37 @@ def tile_transformerblocktpu_pb_kernel(
                 ),
             )
             wo_raw.append(raw)
+        attn_sb = keep.tile([P, TOKEN_TILES, D_MODEL], BF16)
+        for i in range(TOKEN_TILES):
+            nc.sync.dma_start(out=attn_sb[:, i, :], in_=attn_rows[i * P : (i + 1) * P, :])
         x_sb = keep.tile([P, TOKEN_TILES, D_MODEL], BF16)
         nc.sync.dma_start(out=x_sb[:], in_=x_rows.rearrange("(i p) d -> p i d", p=P))
+        load_pair(0)
+        load_pair(1)
+
+        gain_all = consts.tile([P, D_MODEL], BF16)
+        for half in range(D_MODEL // N_TILE):
+            cols = slice(half * N_TILE, (half + 1) * N_TILE)
+            gain_ps = acc.tile([P, N_TILE], F32, tag="acc")
+            nc.tensor.matmul(
+                out=gain_ps[:], lhsT=ones[:], rhs=gain_row[:, cols], start=True, stop=True
+            )
+            nc.scalar.copy(out=gain_all[:, cols], in_=gain_ps[:])
+
+        wo_codes = keep.tile([P, PASSES, D_MODEL], U32, align_bytes=64)
+        wo_scales = keep.tile([P, PASSES, D_MODEL], U8, align_bytes=64)
+        for g in range(PASSES):
+            by_vector = stage.tile([P, N_TILE, PACK], BF16, align_bytes=64)
+            regroup(nc.vector.tensor_copy, by_vector[:], wo_raw[g][:, :, 0:N_TILE])
+            by_scalar = stage.tile([P, N_TILE, PACK], BF16, align_bytes=64)
+            regroup(nc.scalar.copy, by_scalar[:], wo_raw[g][:, :, N_TILE : 2 * N_TILE])
+            for half, tile_ in enumerate((by_vector, by_scalar)):
+                cols = slice(half * N_TILE, (half + 1) * N_TILE)
+                nc.vector.quantize_mx(
+                    out=wo_codes[:, g, cols].bitcast(FP8X4),
+                    scales=wo_scales[:, g, cols],
+                    in_=tile_[:].rearrange("p n t -> p (n t)"),
+                )
 
         a_grouped = keep.tile([P, TOKEN_TILES, PASSES, P, PACK], BF16, align_bytes=64)
         a_codes = keep.tile([P, TOKEN_TILES, PASSES, P], U32, align_bytes=64)
@@ -107,40 +188,22 @@ def tile_transformerblocktpu_pb_kernel(
                 out=a_grouped[:, i].bitcast(F32),
                 in_=at[:].rearrange("q g u r -> q g r u"),
             )
-        nc.vector.quantize_mx(
-            out=a_codes[:].rearrange("q i g r -> q (i g r)").bitcast(FP8X4),
-            scales=a_scales[:].rearrange("q i g r -> q (i g r)"),
-            in_=a_grouped[:].rearrange("q i g r t -> q (i g r t)"),
-        )
-
-        wo_codes = keep.tile([P, PASSES, D_MODEL], U32, align_bytes=64)
-        wo_scales = keep.tile([P, PASSES, D_MODEL], U8, align_bytes=64)
-        for g in range(PASSES):
-            for half in range(D_MODEL // N_TILE):
-                cols = slice(half * N_TILE, (half + 1) * N_TILE)
-                quantise_weight_cols(
-                    nc,
-                    stage,
-                    wo_raw[g][:, :, cols],
-                    wo_codes[:, g, cols],
-                    wo_scales[:, g, cols],
-                    nc.vector.tensor_copy if (g + half) % 2 == 0 else nc.scalar.copy,
-                )
-
-        ones = consts.tile([P, P], BF16)
-        nc.vector.memset(ones[:], 1.0)
-        gain_all = consts.tile([P, D_MODEL], BF16)
-        for half in range(D_MODEL // N_TILE):
-            cols = slice(half * N_TILE, (half + 1) * N_TILE)
-            gain_ps = acc.tile([P, N_TILE], F32, tag="acc")
-            nc.tensor.matmul(
-                out=gain_ps[:], lhsT=ones[:], rhs=gain_row[:, cols], start=True, stop=True
+            nc.vector.quantize_mx(
+                out=a_codes[:, i].rearrange("q g r -> q (g r)").bitcast(FP8X4),
+                scales=a_scales[:, i].rearrange("q g r -> q (g r)"),
+                in_=a_grouped[:, i].rearrange("q g r t -> q (g r t)"),
             )
-            nc.scalar.copy(out=gain_all[:, cols], in_=gain_ps[:])
 
         xmid = keep.tile([P, TOKEN_TILES, D_MODEL], F32)
         sumsq = keep.tile([P, TOKEN_TILES], F32)
-        for i in range(TOKEN_TILES):
+        rms = keep.tile([P, TOKEN_TILES], F32)
+        inv_rms = keep.tile([P, TOKEN_TILES], F32)
+        h_codes = keep.tile([P, TOKEN_TILES, PASSES, P], U32, align_bytes=64)
+        h_scales = keep.tile([P, TOKEN_TILES, PASSES, P], U8, align_bytes=64)
+        xm_banks = {}
+        h_groups = {}
+
+        def first_product(i):
             for half in range(D_MODEL // N_TILE):
                 cols = slice(half * N_TILE, (half + 1) * N_TILE)
                 xm_ps = acc.tile([P, N_TILE], F32, tag="acc")
@@ -154,25 +217,29 @@ def tile_transformerblocktpu_pb_kernel(
                         start=(g == 0),
                         stop=(g == PASSES - 1),
                     )
+                xm_banks[(i, half)] = xm_ps
+
+        def add_and_square(i):
+            for half in range(D_MODEL // N_TILE):
+                cols = slice(half * N_TILE, (half + 1) * N_TILE)
                 nc.vector.tensor_tensor(
-                    out=xmid[:, i, cols], in0=xm_ps[:], in1=x_sb[:, i, cols], op=ALU.add
+                    out=xmid[:, i, cols], in0=xm_banks[(i, half)][:], in1=x_sb[:, i, cols], op=ALU.add
                 )
             nc.gpsimd.dma_start(out=xmid_rows[i * P : (i + 1) * P, :], in_=xmid[:, i, :])
             squares = rows.tile([P, D_MODEL], BF16)
             nc.scalar.activation(
                 out=squares[:], in_=xmid[:, i, :], func=ACT.Square, accum_out=sumsq[:, i : i + 1]
             )
+            nc.scalar.activation(
+                out=rms[:, i : i + 1],
+                in_=sumsq[:, i : i + 1],
+                func=ACT.Sqrt,
+                scale=1.0 / D_MODEL,
+                bias=eps[:, 0:1],
+            )
 
-        rms = keep.tile([P, TOKEN_TILES], F32)
-        nc.scalar.activation(
-            out=rms[:], in_=sumsq[:], func=ACT.Sqrt, scale=1.0 / D_MODEL, bias=eps[:, 0:1]
-        )
-        inv_rms = keep.tile([P, TOKEN_TILES], F32)
-        nc.vector.reciprocal(out=inv_rms[:], in_=rms[:])
-
-        h_codes = keep.tile([P, TOKEN_TILES, PASSES, P], U32, align_bytes=64)
-        h_scales = keep.tile([P, TOKEN_TILES, PASSES, P], U8, align_bytes=64)
-        for i in range(TOKEN_TILES):
+        def norm_and_transpose(i):
+            nc.vector.reciprocal(out=inv_rms[:, i : i + 1], in_=rms[:, i : i + 1])
             h_bf16 = rows.tile([P, D_MODEL], BF16)
             nc.vector.scalar_tensor_tensor(
                 out=h_bf16[:],
@@ -188,62 +255,69 @@ def tile_transformerblocktpu_pb_kernel(
                     out=ht[:, j, :], in_=h_bf16[:, j * P : (j + 1) * P], identity=ident_bf16[:]
                 )
             h_grouped = rows.tile([P, PASSES, P, PACK], BF16, align_bytes=64)
-            nc.scalar.copy(
-                out=h_grouped[:], in_=ht[:].rearrange("p (g t) r -> p g r t", t=PACK)
-            )
+            nc.scalar.copy(out=h_grouped[:], in_=ht[:].rearrange("p (g t) r -> p g r t", t=PACK))
+            h_groups[i] = h_grouped
+
+        def quantise_h(i):
             nc.vector.quantize_mx(
                 out=h_codes[:, i].rearrange("p g r -> p (g r)").bitcast(FP8X4),
                 scales=h_scales[:, i].rearrange("p g r -> p (g r)"),
-                in_=h_grouped[:].rearrange("p g r t -> p (g r t)"),
+                in_=h_groups[i][:].rearrange("p g r t -> p (g r t)"),
             )
 
-        for pair in range(D_FF // LOAD_COLS):
-            raws = []
-            for w in (w_gate, w_up):
-                for g in range(PASSES):
-                    raw = raw_pool.tile([P, PACK, LOAD_COLS], BF16, tag="raw")
-                    nc.sync.dma_start(
-                        out=raw[:],
-                        in_=w[
-                            g * K_PASS : (g + 1) * K_PASS,
-                            pair * LOAD_COLS : (pair + 1) * LOAD_COLS,
-                        ].rearrange("(t p) n -> p t n", p=P),
-                    )
-                    raws.append(raw)
-            for half in range(LOAD_COLS // N_TILE):
-                cols = slice(half * N_TILE, (half + 1) * N_TILE)
-                first_col = pair * LOAD_COLS + half * N_TILE
-                w_codes = codes_pool.tile([P, 2, PASSES, N_TILE], U32, align_bytes=64)
-                w_scales = codes_pool.tile([P, 2, PASSES, N_TILE], U8, align_bytes=64)
-                for m in range(2):
+        for i in range(TOKEN_TILES):
+            first_product(i)
+            if i >= 2:
+                add_and_square(i - 2)
+        for i in range(TOKEN_TILES):
+            norm_and_transpose(i)
+            if i + 2 < TOKEN_TILES:
+                add_and_square(i + 2)
+            if i >= 1:
+                quantise_h(i - 1)
+            scalar_regroup(0, i)
+            if i == 2:
+                vector_regroup(0, GATE)
+        nc.scalar.activation(out=warm[:, 1:2], in_=eps[:], func=ACT.Silu)
+        vector_regroup(0, UP)
+        quantise(0, GATE, 0)
+        quantise_h(TOKEN_TILES - 1)
+        quantise(0, GATE, 1)
+        quantise(0, UP, 0)
+        quantise(0, UP, 1)
+
+        for chunk in range(CHUNKS):
+            if chunk % 2 == 0 and chunk // 2 + 2 < PAIRS:
+                load_pair(chunk // 2 + 2)
+            for i in range(TOKEN_TILES):
+                gate_ps = acc.tile([P, N_TILE], F32, tag="acc")
+                up_ps = acc.tile([P, N_TILE], F32, tag="acc")
+                for m, product in enumerate((gate_ps, up_ps)):
                     for g in range(PASSES):
-                        quantise_weight_cols(
-                            nc,
-                            stage,
-                            raws[m * PASSES + g][:, :, cols],
-                            w_codes[:, m, g, :],
-                            w_scales[:, m, g, :],
-                            nc.vector.tensor_copy if (g + m) % 2 == 0 else nc.scalar.copy,
+                        nc.tensor.matmul_mx(
+                            out=product[:],
+                            lhsT=h_codes[:, i, g, :].bitcast(FP8X4),
+                            lhsT_scale=h_scales[:, i, g, :],
+                            rhs=w_codes[chunk][:, m, g, :].bitcast(FP8X4),
+                            rhs_scale=w_scales[chunk][:, m, g, :],
+                            start=(g == 0),
+                            stop=(g == PASSES - 1),
                         )
-                for i in range(TOKEN_TILES):
-                    gate_ps = acc.tile([P, N_TILE], F32, tag="acc")
-                    up_ps = acc.tile([P, N_TILE], F32, tag="acc")
-                    for m, product in enumerate((gate_ps, up_ps)):
-                        for g in range(PASSES):
-                            nc.tensor.matmul_mx(
-                                out=product[:],
-                                lhsT=h_codes[:, i, g, :].bitcast(FP8X4),
-                                lhsT_scale=h_scales[:, i, g, :],
-                                rhs=w_codes[:, m, g, :].bitcast(FP8X4),
-                                rhs_scale=w_scales[:, m, g, :],
-                                start=(g == 0),
-                                stop=(g == PASSES - 1),
-                            )
-                    silu = ep.tile([P, N_TILE], F32)
-                    nc.scalar.activation(out=silu[:], in_=gate_ps[:], func=ACT.Silu)
-                    g_sb = out_pool.tile([P, N_TILE], F32)
-                    nc.vector.tensor_tensor(out=g_sb[:], in0=up_ps[:], in1=silu[:], op=ALU.mult)
-                    nc.gpsimd.dma_start(
-                        out=g_rows[i * P : (i + 1) * P, first_col : first_col + N_TILE],
-                        in_=g_sb[:],
-                    )
+                scalar_regroup(chunk + 1, i)
+                silu = ep.tile([P, N_TILE], F32)
+                nc.scalar.activation(out=silu[:], in_=gate_ps[:], func=ACT.Silu)
+                if i == 0:
+                    vector_regroup(chunk + 1, GATE)
+                    vector_regroup(chunk + 1, UP)
+                if i == 2:
+                    quantise(chunk + 1, GATE, 0)
+                    quantise(chunk + 1, UP, 0)
+                    quantise(chunk + 1, GATE, 1)
+                if i == 3:
+                    quantise(chunk + 1, UP, 1)
+                g_sb = out_pool.tile([P, N_TILE], F32)
+                nc.vector.tensor_tensor(out=g_sb[:], in0=up_ps[:], in1=silu[:], op=ALU.mult)
+                first_col = chunk * N_TILE
+                nc.gpsimd.dma_start(
+                    out=g_rows[i * P : (i + 1) * P, first_col : first_col + N_TILE], in_=g_sb[:]
+                )

@@ -225,7 +225,7 @@ def tile_transformerblocktpu_pb_kernel(
                 nc.vector.tensor_tensor(
                     out=xmid[:, i, cols], in0=xm_banks[(i, half)][:], in1=x_sb[:, i, cols], op=ALU.add
                 )
-            nc.gpsimd.dma_start(out=xmid_rows[i * P : (i + 1) * P, :], in_=xmid[:, i, :])
+            nc.sync.dma_start(out=xmid_rows[i * P : (i + 1) * P, :], in_=xmid[:, i, :])
             squares = rows.tile([P, D_MODEL], BF16)
             nc.scalar.activation(
                 out=squares[:], in_=xmid[:, i, :], func=ACT.Square, accum_out=sumsq[:, i : i + 1]
@@ -287,8 +287,6 @@ def tile_transformerblocktpu_pb_kernel(
         quantise(0, UP, 1)
 
         for chunk in range(CHUNKS):
-            if chunk % 2 == 0 and chunk // 2 + 2 < PAIRS:
-                load_pair(chunk // 2 + 2)
             for i in range(TOKEN_TILES):
                 gate_ps = acc.tile([P, N_TILE], F32, tag="acc")
                 up_ps = acc.tile([P, N_TILE], F32, tag="acc")
@@ -318,6 +316,8 @@ def tile_transformerblocktpu_pb_kernel(
                 g_sb = out_pool.tile([P, N_TILE], F32)
                 nc.vector.tensor_tensor(out=g_sb[:], in0=up_ps[:], in1=silu[:], op=ALU.mult)
                 first_col = chunk * N_TILE
-                nc.gpsimd.dma_start(
+                nc.sync.dma_start(
                     out=g_rows[i * P : (i + 1) * P, first_col : first_col + N_TILE], in_=g_sb[:]
                 )
+            if chunk % 2 == 0 and chunk // 2 + 2 < PAIRS:
+                load_pair(chunk // 2 + 2)

@@ -20,10 +20,15 @@ D_FF = 4096
 TOKEN_TILES = TOKENS // P
 PASSES = D_MODEL // K_PASS
 N_TILE = 512
+HALVES = D_MODEL // N_TILE
 CHUNKS = D_FF // N_TILE
+STEPS = CHUNKS * TOKEN_TILES
 LOAD_COLS = 2 * N_TILE
-PAIRS = D_FF // LOAD_COLS
+UNITS = 2 * PASSES * (D_FF // LOAD_COLS)
+RAW_BUFS = 9
+PARTS = 4
 PIECE = N_TILE // 2
+LEAD = 7
 RUN = 4
 GATE, UP = 0, 1
 EPS = 1e-6
@@ -50,14 +55,13 @@ def tile_transformerblocktpu_pb_kernel(
     with ExitStack() as ctx:
         consts = ctx.enter_context(tc.tile_pool(name="consts", bufs=1))
         keep = ctx.enter_context(tc.tile_pool(name="keep", bufs=1))
-        raw_pool = ctx.enter_context(tc.tile_pool(name="raw", bufs=9))
+        raw_pool = ctx.enter_context(tc.tile_pool(name="raw", bufs=RAW_BUFS))
         stage = ctx.enter_context(tc.tile_pool(name="stage", bufs=3))
         rows = ctx.enter_context(tc.tile_pool(name="rows", bufs=2))
         codes_pool = ctx.enter_context(tc.tile_pool(name="codes", bufs=3))
         ep = ctx.enter_context(tc.tile_pool(name="ep", bufs=3))
         out_pool = ctx.enter_context(tc.tile_pool(name="out", bufs=8))
-        acc = ctx.enter_context(tc.psum_pool(name="acc", bufs=6))
-        tp = ctx.enter_context(tc.psum_pool(name="tp", bufs=2))
+        banks = ctx.enter_context(tc.psum_pool(name="banks", bufs=8))
         ctx.enter_context(tc.manual_schedule())
 
         raws = {}
@@ -65,69 +69,80 @@ def tile_transformerblocktpu_pb_kernel(
         w_codes = {}
         w_scales = {}
 
-        def load_pair(pair):
-            for m, w in enumerate((w_gate, w_up)):
-                for g in range(PASSES):
-                    raw = raw_pool.tile([P, PACK, LOAD_COLS], BF16, tag="raw")
-                    nc.sync.dma_start(
-                        out=raw[:],
-                        in_=w[
-                            g * K_PASS : (g + 1) * K_PASS,
-                            pair * LOAD_COLS : (pair + 1) * LOAD_COLS,
-                        ].rearrange("(t p) n -> p t n", p=P),
-                    )
-                    raws[(pair, m, g)] = raw
+        def load_unit(unit):
+            pair, rest = divmod(unit, 2 * PASSES)
+            m, g = divmod(rest, PASSES)
+            w = (w_gate, w_up)[m]
+            raw = raw_pool.tile([P, PACK, LOAD_COLS], BF16, tag="raw")
+            nc.sync.dma_start(
+                out=raw[:],
+                in_=w[
+                    g * K_PASS : (g + 1) * K_PASS, pair * LOAD_COLS : (pair + 1) * LOAD_COLS
+                ].rearrange("(t p) n -> p t n", p=P),
+            )
+            raws[unit] = raw
 
         def raw_cols(chunk, m, g, first, width):
             start = (chunk % 2) * N_TILE + first
-            return raws[(chunk // 2, m, g)][:, :, start : start + width]
+            unit = (chunk // 2) * 2 * PASSES + m * PASSES + g
+            return raws[unit][:, :, start : start + width]
 
-        def vector_regroup(chunk, m):
-            if chunk < CHUNKS:
-                by_vector = stage.tile([P, N_TILE, PACK], BF16, align_bytes=64)
-                regroup(nc.vector.tensor_copy, by_vector[:], raw_cols(chunk, m, 0, 0, N_TILE))
-                grouped[(chunk, m, 0)] = by_vector
+        def quantise(chunk, m, g):
+            nc.vector.quantize_mx(
+                out=w_codes[chunk][:, m, g, :].bitcast(FP8X4),
+                scales=w_scales[chunk][:, m, g, :],
+                in_=grouped[(chunk, m, g)][:].rearrange("p n t -> p (n t)"),
+            )
 
-        def scalar_regroup(chunk, piece):
+        def scalar_regroup(index):
+            chunk, piece = divmod(index, PARTS)
             if chunk < CHUNKS:
-                m, part = divmod(piece, 2)
-                if part == 0:
+                m, side = divmod(piece, 2)
+                if side == 0:
                     by_scalar = stage.tile([P, N_TILE, PACK], BF16, align_bytes=64)
                     grouped[(chunk, m, 1)] = by_scalar
-                first = part * PIECE
+                first = side * PIECE
                 regroup(
                     nc.scalar.copy,
                     grouped[(chunk, m, 1)][:, first : first + PIECE, :],
                     raw_cols(chunk, m, 1, first, PIECE),
                 )
 
-        def quantise(chunk, m, g):
+        def vector_prepare(index):
+            chunk, part = divmod(index, PARTS)
             if chunk < CHUNKS:
-                if chunk not in w_codes:
+                if part < 2:
+                    by_vector = stage.tile([P, N_TILE, PACK], BF16, align_bytes=64)
+                    regroup(nc.vector.tensor_copy, by_vector[:], raw_cols(chunk, part, 0, 0, N_TILE))
+                    grouped[(chunk, part, 0)] = by_vector
+                if part == 2:
                     codes = codes_pool.tile([P, 2, PASSES, N_TILE], U32, align_bytes=64)
                     scales = codes_pool.tile([P, 2, PASSES, N_TILE], U8, align_bytes=64)
                     w_codes[chunk] = codes
                     w_scales[chunk] = scales
-                nc.vector.quantize_mx(
-                    out=w_codes[chunk][:, m, g, :].bitcast(FP8X4),
-                    scales=w_scales[chunk][:, m, g, :],
-                    in_=grouped[(chunk, m, g)][:].rearrange("p n t -> p (n t)"),
-                )
+                    quantise(chunk, GATE, 0)
+                    quantise(chunk, UP, 0)
+                if part == 3:
+                    quantise(chunk, GATE, 1)
+                    quantise(chunk, UP, 1)
+                    if chunk % 2 == 1:
+                        freed = (chunk // 2) * 2 * PASSES
+                        for unit in range(freed + RAW_BUFS, min(freed + RAW_BUFS + 4, UNITS)):
+                            load_unit(unit)
 
-        eps = consts.tile([P, 1], F32)
-        nc.vector.memset(eps[:], EPS)
         gain_row = consts.tile([P, D_MODEL], BF16)
         nc.vector.memset(gain_row[:], 0.0)
+        neg_half = consts.tile([P, 1], F32)
+        nc.vector.memset(neg_half[:], -0.5)
         ones = consts.tile([P, P], BF16)
         nc.vector.memset(ones[:], 1.0)
-        warm = consts.tile([P, 2], F32)
-        nc.scalar.activation(out=warm[:, 0:1], in_=eps[:], func=ACT.Sqrt)
+        warm = consts.tile([P, 1], F32)
+        nc.scalar.activation(out=warm[:], in_=neg_half[:], func=ACT.Silu)
         ident_f32 = consts.tile([P, P], F32)
         make_identity(nc, ident_f32[:])
         ident_bf16 = consts.tile([P, P], BF16)
         make_identity(nc, ident_bf16[:])
 
-        nc.sync.dma_start(out=gain_row[0:1, :], in_=rms2_scale.unsqueeze(0))
         wo_raw = []
         for g in range(PASSES):
             raw = raw_pool.tile([P, PACK, LOAD_COLS], BF16, tag="raw")
@@ -138,22 +153,28 @@ def tile_transformerblocktpu_pb_kernel(
                 ),
             )
             wo_raw.append(raw)
+            if g == 0:
+                nc.sync.dma_start(out=gain_row[0:1, :], in_=rms2_scale.unsqueeze(0))
         attn_sb = keep.tile([P, TOKEN_TILES, D_MODEL], BF16)
         for i in range(TOKEN_TILES):
             nc.sync.dma_start(out=attn_sb[:, i, :], in_=attn_rows[i * P : (i + 1) * P, :])
         x_sb = keep.tile([P, TOKEN_TILES, D_MODEL], BF16)
-        nc.sync.dma_start(out=x_sb[:], in_=x_rows.rearrange("(i p) d -> p i d", p=P))
-        load_pair(0)
-        load_pair(1)
+        for i in range(TOKEN_TILES):
+            nc.sync.dma_start(out=x_sb[:, i, :], in_=x_rows[i * P : (i + 1) * P, :])
+        for unit in range(RAW_BUFS):
+            load_unit(unit)
 
-        gain_all = consts.tile([P, D_MODEL], BF16)
-        for half in range(D_MODEL // N_TILE):
-            cols = slice(half * N_TILE, (half + 1) * N_TILE)
-            gain_ps = acc.tile([P, N_TILE], F32, tag="acc")
+        gain_banks = []
+        for half in range(HALVES):
+            gain_ps = banks.tile([P, N_TILE], F32, tag="bank")
             nc.tensor.matmul(
-                out=gain_ps[:], lhsT=ones[:], rhs=gain_row[:, cols], start=True, stop=True
+                out=gain_ps[:],
+                lhsT=ones[:],
+                rhs=gain_row[:, half * N_TILE : (half + 1) * N_TILE],
+                start=True,
+                stop=True,
             )
-            nc.scalar.copy(out=gain_all[:, cols], in_=gain_ps[:])
+            gain_banks.append(gain_ps)
 
         wo_codes = keep.tile([P, PASSES, D_MODEL], U32, align_bytes=64)
         wo_scales = keep.tile([P, PASSES, D_MODEL], U8, align_bytes=64)
@@ -175,7 +196,7 @@ def tile_transformerblocktpu_pb_kernel(
         a_scales = keep.tile([P, TOKEN_TILES, PASSES, P], U8, align_bytes=64)
         for i in range(TOKEN_TILES):
             attn_words = attn_sb[:, i, :].bitcast(F32)
-            at = tp.tile([P, PASSES, 2, P], F32, tag="tp")
+            at = banks.tile([P, PASSES, 2, P], F32, tag="bank")
             for g in range(PASSES):
                 for u in range(2):
                     first = (2 * g + u) * P
@@ -194,19 +215,27 @@ def tile_transformerblocktpu_pb_kernel(
                 in_=a_grouped[:, i].rearrange("q g r t -> q (g r t)"),
             )
 
+        gain_all = consts.tile([P, D_MODEL], BF16)
+        for half in range(HALVES):
+            nc.scalar.mul(
+                out=gain_all[:, half * N_TILE : (half + 1) * N_TILE],
+                in_=gain_banks[half][:],
+                mul=D_MODEL**0.5,
+            )
+
         xmid = keep.tile([P, TOKEN_TILES, D_MODEL], F32)
         sumsq = keep.tile([P, TOKEN_TILES], F32)
-        rms = keep.tile([P, TOKEN_TILES], F32)
-        inv_rms = keep.tile([P, TOKEN_TILES], F32)
+        shifted = keep.tile([P, TOKEN_TILES], F32)
+        inv_norm = keep.tile([P, TOKEN_TILES], F32)
         h_codes = keep.tile([P, TOKEN_TILES, PASSES, P], U32, align_bytes=64)
         h_scales = keep.tile([P, TOKEN_TILES, PASSES, P], U8, align_bytes=64)
         xm_banks = {}
         h_groups = {}
 
         def first_product(i):
-            for half in range(D_MODEL // N_TILE):
+            for half in range(HALVES):
                 cols = slice(half * N_TILE, (half + 1) * N_TILE)
-                xm_ps = acc.tile([P, N_TILE], F32, tag="acc")
+                xm_ps = banks.tile([P, N_TILE], F32, tag="bank")
                 for g in range(PASSES):
                     nc.tensor.matmul_mx(
                         out=xm_ps[:],
@@ -220,7 +249,8 @@ def tile_transformerblocktpu_pb_kernel(
                 xm_banks[(i, half)] = xm_ps
 
         def add_and_square(i):
-            for half in range(D_MODEL // N_TILE):
+            one = slice(i, i + 1)
+            for half in range(HALVES):
                 cols = slice(half * N_TILE, (half + 1) * N_TILE)
                 nc.vector.tensor_tensor(
                     out=xmid[:, i, cols], in0=xm_banks[(i, half)][:], in1=x_sb[:, i, cols], op=ALU.add
@@ -228,28 +258,31 @@ def tile_transformerblocktpu_pb_kernel(
             nc.sync.dma_start(out=xmid_rows[i * P : (i + 1) * P, :], in_=xmid[:, i, :])
             squares = rows.tile([P, D_MODEL], BF16)
             nc.scalar.activation(
-                out=squares[:], in_=xmid[:, i, :], func=ACT.Square, accum_out=sumsq[:, i : i + 1]
+                out=squares[:], in_=xmid[:, i, :], func=ACT.Square, accum_out=sumsq[:, one]
             )
-            nc.scalar.activation(
-                out=rms[:, i : i + 1],
-                in_=sumsq[:, i : i + 1],
-                func=ACT.Sqrt,
-                scale=1.0 / D_MODEL,
-                bias=eps[:, 0:1],
+            nc.gpsimd.tensor_scalar(
+                out=shifted[:, one],
+                in0=sumsq[:, one],
+                scalar1=D_MODEL * EPS,
+                scalar2=1.0,
+                op0=ALU.add,
+                op1=ALU.mult,
+            )
+            nc.gpsimd.tensor_tensor(
+                out=inv_norm[:, one], in0=shifted[:, one], in1=neg_half[:], op=ALU.pow
             )
 
         def norm_and_transpose(i):
-            nc.vector.reciprocal(out=inv_rms[:, i : i + 1], in_=rms[:, i : i + 1])
             h_bf16 = rows.tile([P, D_MODEL], BF16)
             nc.vector.scalar_tensor_tensor(
                 out=h_bf16[:],
                 in0=xmid[:, i, :],
-                scalar=inv_rms[:, i : i + 1],
+                scalar=inv_norm[:, i : i + 1],
                 in1=gain_all[:],
                 op0=ALU.mult,
                 op1=ALU.mult,
             )
-            ht = tp.tile([P, PASSES * PACK, P], BF16, tag="tp")
+            ht = banks.tile([P, PASSES * PACK, P], BF16, tag="bank")
             for j in range(PASSES * PACK):
                 nc.tensor.transpose(
                     out=ht[:, j, :], in_=h_bf16[:, j * P : (j + 1) * P], identity=ident_bf16[:]
@@ -267,57 +300,44 @@ def tile_transformerblocktpu_pb_kernel(
 
         for i in range(TOKEN_TILES):
             first_product(i)
-            if i >= 2:
-                add_and_square(i - 2)
+            if i >= 1:
+                add_and_square(i - 1)
         for i in range(TOKEN_TILES):
             norm_and_transpose(i)
-            if i + 2 < TOKEN_TILES:
-                add_and_square(i + 2)
+            if i == 0:
+                add_and_square(TOKEN_TILES - 1)
+            vector_prepare(i)
             if i >= 1:
                 quantise_h(i - 1)
-            scalar_regroup(0, i)
-            if i == 2:
-                vector_regroup(0, GATE)
-        nc.scalar.activation(out=warm[:, 1:2], in_=eps[:], func=ACT.Silu)
-        vector_regroup(0, UP)
-        quantise(0, GATE, 0)
+                scalar_regroup(2 * i - 1)
+            scalar_regroup(2 * i)
+        vector_prepare(TOKEN_TILES)
         quantise_h(TOKEN_TILES - 1)
-        quantise(0, GATE, 1)
-        quantise(0, UP, 0)
-        quantise(0, UP, 1)
+        for index in range(TOKEN_TILES + 1, LEAD):
+            vector_prepare(index)
 
-        for chunk in range(CHUNKS):
-            for i in range(TOKEN_TILES):
-                gate_ps = acc.tile([P, N_TILE], F32, tag="acc")
-                up_ps = acc.tile([P, N_TILE], F32, tag="acc")
-                for m, product in enumerate((gate_ps, up_ps)):
-                    for g in range(PASSES):
-                        nc.tensor.matmul_mx(
-                            out=product[:],
-                            lhsT=h_codes[:, i, g, :].bitcast(FP8X4),
-                            lhsT_scale=h_scales[:, i, g, :],
-                            rhs=w_codes[chunk][:, m, g, :].bitcast(FP8X4),
-                            rhs_scale=w_scales[chunk][:, m, g, :],
-                            start=(g == 0),
-                            stop=(g == PASSES - 1),
-                        )
-                scalar_regroup(chunk + 1, i)
-                silu = ep.tile([P, N_TILE], F32)
-                nc.scalar.activation(out=silu[:], in_=gate_ps[:], func=ACT.Silu)
-                if i == 0:
-                    vector_regroup(chunk + 1, GATE)
-                    vector_regroup(chunk + 1, UP)
-                if i == 2:
-                    quantise(chunk + 1, GATE, 0)
-                    quantise(chunk + 1, UP, 0)
-                    quantise(chunk + 1, GATE, 1)
-                if i == 3:
-                    quantise(chunk + 1, UP, 1)
-                g_sb = out_pool.tile([P, N_TILE], F32)
-                nc.vector.tensor_tensor(out=g_sb[:], in0=up_ps[:], in1=silu[:], op=ALU.mult)
-                first_col = chunk * N_TILE
-                nc.sync.dma_start(
-                    out=g_rows[i * P : (i + 1) * P, first_col : first_col + N_TILE], in_=g_sb[:]
-                )
-            if chunk % 2 == 0 and chunk // 2 + 2 < PAIRS:
-                load_pair(chunk // 2 + 2)
+        for step in range(STEPS):
+            chunk, i = divmod(step, TOKEN_TILES)
+            gate_ps = banks.tile([P, N_TILE], F32, tag="bank")
+            up_ps = banks.tile([P, N_TILE], F32, tag="bank")
+            for m, product in enumerate((gate_ps, up_ps)):
+                for g in range(PASSES):
+                    nc.tensor.matmul_mx(
+                        out=product[:],
+                        lhsT=h_codes[:, i, g, :].bitcast(FP8X4),
+                        lhsT_scale=h_scales[:, i, g, :],
+                        rhs=w_codes[chunk][:, m, g, :].bitcast(FP8X4),
+                        rhs_scale=w_scales[chunk][:, m, g, :],
+                        start=(g == 0),
+                        stop=(g == PASSES - 1),
+                    )
+            scalar_regroup(step + LEAD)
+            silu = ep.tile([P, N_TILE], F32)
+            nc.scalar.activation(out=silu[:], in_=gate_ps[:], func=ACT.Silu)
+            vector_prepare(step + LEAD)
+            g_sb = out_pool.tile([P, N_TILE], F32)
+            nc.vector.tensor_tensor(out=g_sb[:], in0=up_ps[:], in1=silu[:], op=ALU.mult)
+            first_col = chunk * N_TILE
+            nc.sync.dma_start(
+                out=g_rows[i * P : (i + 1) * P, first_col : first_col + N_TILE], in_=g_sb[:]
+            )

@@ -30,7 +30,6 @@ PARTS = 4
 PIECE = N_TILE // 2
 LEAD = 7
 RUN = 4
-GATE, UP = 0, 1
 EPS = 1e-6
 
 FLOPS = 2 * TOKENS * D_MODEL * (D_MODEL + 2 * D_FF)
@@ -56,7 +55,7 @@ def tile_transformerblocktpu_pb_kernel(
         consts = ctx.enter_context(tc.tile_pool(name="consts", bufs=1))
         keep = ctx.enter_context(tc.tile_pool(name="keep", bufs=1))
         raw_pool = ctx.enter_context(tc.tile_pool(name="raw", bufs=RAW_BUFS))
-        stage = ctx.enter_context(tc.tile_pool(name="stage", bufs=3))
+        stage = ctx.enter_context(tc.tile_pool(name="stage", bufs=2))
         rows = ctx.enter_context(tc.tile_pool(name="rows", bufs=2))
         codes_pool = ctx.enter_context(tc.tile_pool(name="codes", bufs=3))
         ep = ctx.enter_context(tc.tile_pool(name="ep", bufs=3))
@@ -87,48 +86,50 @@ def tile_transformerblocktpu_pb_kernel(
             unit = (chunk // 2) * 2 * PASSES + m * PASSES + g
             return raws[unit][:, :, start : start + width]
 
-        def quantise(chunk, m, g):
+        def quantise(chunk, g):
             nc.vector.quantize_mx(
-                out=w_codes[chunk][:, m, g, :].bitcast(FP8X4),
-                scales=w_scales[chunk][:, m, g, :],
-                in_=grouped[(chunk, m, g)][:].rearrange("p n t -> p (n t)"),
+                out=w_codes[chunk][:, g].rearrange("p m n -> p (m n)").bitcast(FP8X4),
+                scales=w_scales[chunk][:, g].rearrange("p m n -> p (m n)"),
+                in_=grouped[(chunk, g)][:].rearrange("p m n t -> p (m n t)"),
             )
 
         def scalar_regroup(index):
             chunk, piece = divmod(index, PARTS)
             if chunk < CHUNKS:
+                if piece == 0:
+                    by_scalar = stage.tile([P, 2, N_TILE, PACK], BF16, align_bytes=64)
+                    grouped[(chunk, 1)] = by_scalar
                 m, side = divmod(piece, 2)
-                if side == 0:
-                    by_scalar = stage.tile([P, N_TILE, PACK], BF16, align_bytes=64)
-                    grouped[(chunk, m, 1)] = by_scalar
                 first = side * PIECE
                 regroup(
                     nc.scalar.copy,
-                    grouped[(chunk, m, 1)][:, first : first + PIECE, :],
+                    grouped[(chunk, 1)][:, m, first : first + PIECE, :],
                     raw_cols(chunk, m, 1, first, PIECE),
                 )
 
         def vector_prepare(index):
             chunk, part = divmod(index, PARTS)
             if chunk < CHUNKS:
+                if part == 0:
+                    by_vector = stage.tile([P, 2, N_TILE, PACK], BF16, align_bytes=64)
+                    grouped[(chunk, 0)] = by_vector
                 if part < 2:
-                    by_vector = stage.tile([P, N_TILE, PACK], BF16, align_bytes=64)
-                    regroup(nc.vector.tensor_copy, by_vector[:], raw_cols(chunk, part, 0, 0, N_TILE))
-                    grouped[(chunk, part, 0)] = by_vector
+                    regroup(
+                        nc.vector.tensor_copy,
+                        grouped[(chunk, 0)][:, part],
+                        raw_cols(chunk, part, 0, 0, N_TILE),
+                    )
                 if part == 2:
-                    codes = codes_pool.tile([P, 2, PASSES, N_TILE], U32, align_bytes=64)
-                    scales = codes_pool.tile([P, 2, PASSES, N_TILE], U8, align_bytes=64)
+                    codes = codes_pool.tile([P, PASSES, 2, N_TILE], U32, align_bytes=64)
+                    scales = codes_pool.tile([P, PASSES, 2, N_TILE], U8, align_bytes=64)
                     w_codes[chunk] = codes
                     w_scales[chunk] = scales
-                    quantise(chunk, GATE, 0)
-                    quantise(chunk, UP, 0)
+                    quantise(chunk, 0)
                 if part == 3:
-                    quantise(chunk, GATE, 1)
-                    quantise(chunk, UP, 1)
-                    if chunk % 2 == 1:
-                        freed = (chunk // 2) * 2 * PASSES
-                        for unit in range(freed + RAW_BUFS, min(freed + RAW_BUFS + 4, UNITS)):
-                            load_unit(unit)
+                    quantise(chunk, 1)
+                refill = (chunk // 2) * 2 * PASSES + part + RAW_BUFS
+                if chunk % 2 == 1 and refill < UNITS:
+                    load_unit(refill)
 
         gain_row = consts.tile([P, D_MODEL], BF16)
         nc.vector.memset(gain_row[:], 0.0)
@@ -178,17 +179,17 @@ def tile_transformerblocktpu_pb_kernel(
 
         wo_codes = keep.tile([P, PASSES, D_MODEL], U32, align_bytes=64)
         wo_scales = keep.tile([P, PASSES, D_MODEL], U8, align_bytes=64)
+        by_vector = stage.tile([P, PASSES, N_TILE, PACK], BF16, align_bytes=64)
+        by_scalar = stage.tile([P, PASSES, N_TILE, PACK], BF16, align_bytes=64)
         for g in range(PASSES):
-            by_vector = stage.tile([P, N_TILE, PACK], BF16, align_bytes=64)
-            regroup(nc.vector.tensor_copy, by_vector[:], wo_raw[g][:, :, 0:N_TILE])
-            by_scalar = stage.tile([P, N_TILE, PACK], BF16, align_bytes=64)
-            regroup(nc.scalar.copy, by_scalar[:], wo_raw[g][:, :, N_TILE : 2 * N_TILE])
+            regroup(nc.vector.tensor_copy, by_vector[:, g], wo_raw[g][:, :, 0:N_TILE])
+            regroup(nc.scalar.copy, by_scalar[:, g], wo_raw[g][:, :, N_TILE : 2 * N_TILE])
             for half, tile_ in enumerate((by_vector, by_scalar)):
                 cols = slice(half * N_TILE, (half + 1) * N_TILE)
                 nc.vector.quantize_mx(
                     out=wo_codes[:, g, cols].bitcast(FP8X4),
                     scales=wo_scales[:, g, cols],
-                    in_=tile_[:].rearrange("p n t -> p (n t)"),
+                    in_=tile_[:, g].rearrange("p n t -> p (n t)"),
                 )
 
         a_grouped = keep.tile([P, TOKEN_TILES, PASSES, P, PACK], BF16, align_bytes=64)
@@ -326,8 +327,8 @@ def tile_transformerblocktpu_pb_kernel(
                         out=product[:],
                         lhsT=h_codes[:, i, g, :].bitcast(FP8X4),
                         lhsT_scale=h_scales[:, i, g, :],
-                        rhs=w_codes[chunk][:, m, g, :].bitcast(FP8X4),
-                        rhs_scale=w_scales[chunk][:, m, g, :],
+                        rhs=w_codes[chunk][:, g, m, :].bitcast(FP8X4),
+                        rhs_scale=w_scales[chunk][:, g, m, :],
                         start=(g == 0),
                         stop=(g == PASSES - 1),
                     )

from contextlib import ExitStack

import concourse.mybir as mybir
from concourse.masks import make_identity

F32 = mybir.dt.float32
BF16 = mybir.dt.bfloat16
U32 = mybir.dt.uint32
U8 = mybir.dt.uint8
FP8X4 = mybir.dt.float8_e4m3fn_x4
ACT = mybir.ActivationFunctionType
ALU = mybir.AluOpType

P = 128
PACK = 4
K_PASS = P * PACK
TOKENS = 512
D_MODEL = 1024
D_FF = 4096
TOKEN_TILES = TOKENS // P
PASSES = D_MODEL // K_PASS
N_TILE = 512
HALVES = D_MODEL // N_TILE
CHUNKS = D_FF // N_TILE
STEPS = CHUNKS * TOKEN_TILES
LOAD_COLS = 2 * N_TILE
UNITS = 2 * PASSES * (D_FF // LOAD_COLS)
RAW_BUFS = 9
PARTS = 4
PIECE = N_TILE // 2
LEAD = 7
RUN = 4
EPS = 1e-6

FLOPS = 2 * TOKENS * D_MODEL * (D_MODEL + 2 * D_FF)


def regroup(copy, grouped_cols, raw_cols):
    copy(
        out=grouped_cols.rearrange("p (c i) t -> p c t i", i=RUN),
        in_=raw_cols.rearrange("p t (c i) -> p c t i", i=RUN),
    )


def tile_transformerblocktpu_pb_kernel(
    tc, attn, x, w_o, rms2_scale, w_gate, w_up, out_0, out_1
):
    nc = tc.nc
    attn_rows = attn.flatten_outer_dims()
    x_rows = x.flatten_outer_dims()
    xmid_rows = out_0.flatten_outer_dims()
    g_rows = out_1.flatten_outer_dims()

    with ExitStack() as ctx:
        consts = ctx.enter_context(tc.tile_pool(name="consts", bufs=1))
        keep = ctx.enter_context(tc.tile_pool(name="keep", bufs=1))
        raw_pool = ctx.enter_context(tc.tile_pool(name="raw", bufs=RAW_BUFS))
        stage = ctx.enter_context(tc.tile_pool(name="stage", bufs=2))
        rows = ctx.enter_context(tc.tile_pool(name="rows", bufs=2))
        codes_pool = ctx.enter_context(tc.tile_pool(name="codes", bufs=3))
        ep = ctx.enter_context(tc.tile_pool(name="ep", bufs=3))
        out_pool = ctx.enter_context(tc.tile_pool(name="out", bufs=8))
        banks = ctx.enter_context(tc.psum_pool(name="banks", bufs=8))
        ctx.enter_context(tc.manual_schedule())

        raws = {}
        grouped = {}
        w_codes = {}
        w_scales = {}

        def load_unit(unit):
            pair, rest = divmod(unit, 2 * PASSES)
            m, g = divmod(rest, PASSES)
            w = (w_gate, w_up)[m]
            raw = raw_pool.tile([P, PACK, LOAD_COLS], BF16, tag="raw")
            nc.sync.dma_start(
                out=raw[:],
                in_=w[
                    g * K_PASS : (g + 1) * K_PASS, pair * LOAD_COLS : (pair + 1) * LOAD_COLS
                ].rearrange("(t p) n -> p t n", p=P),
            )
            raws[unit] = raw

        def raw_cols(chunk, m, g, first, width):
            start = (chunk % 2) * N_TILE + first
            unit = (chunk // 2) * 2 * PASSES + m * PASSES + g
            return raws[unit][:, :, start : start + width]

        def quantise(chunk, g):
            nc.vector.quantize_mx(
                out=w_codes[chunk][:, g].rearrange("p m n -> p (m n)").bitcast(FP8X4),
                scales=w_scales[chunk][:, g].rearrange("p m n -> p (m n)"),
                in_=grouped[(chunk, g)][:].rearrange("p m n t -> p (m n t)"),
            )

        def scalar_regroup(index):
            chunk, piece = divmod(index, PARTS)
            if chunk < CHUNKS:
                if piece == 0:
                    by_scalar = stage.tile([P, 2, N_TILE, PACK], BF16, align_bytes=64)
                    grouped[(chunk, 1)] = by_scalar
                m, side = divmod(piece, 2)
                first = side * PIECE
                regroup(
                    nc.scalar.copy,
                    grouped[(chunk, 1)][:, m, first : first + PIECE, :],
                    raw_cols(chunk, m, 1, first, PIECE),
                )

        def vector_prepare(index):
            chunk, part = divmod(index, PARTS)
            if chunk < CHUNKS:
                if part == 0:
                    by_vector = stage.tile([P, 2, N_TILE, PACK], BF16, align_bytes=64)
                    grouped[(chunk, 0)] = by_vector
                if part < 2:
                    regroup(
                        nc.vector.tensor_copy,
                        grouped[(chunk, 0)][:, part],
                        raw_cols(chunk, part, 0, 0, N_TILE),
                    )
                if part == 2:
                    codes = codes_pool.tile([P, PASSES, 2, N_TILE], U32, align_bytes=64)
                    scales = codes_pool.tile([P, PASSES, 2, N_TILE], U8, align_bytes=64)
                    w_codes[chunk] = codes
                    w_scales[chunk] = scales
                    quantise(chunk, 0)
                if part == 3:
                    quantise(chunk, 1)
                refill = (chunk // 2) * 2 * PASSES + part + RAW_BUFS
                if chunk % 2 == 1 and refill < UNITS:
                    load_unit(refill)

        gain_row = consts.tile([P, D_MODEL], BF16)
        nc.vector.memset(gain_row[:], 0.0)
        neg_half = consts.tile([P, 1], F32)
        nc.vector.memset(neg_half[:], -0.5)
        ones = consts.tile([P, P], BF16)
        nc.vector.memset(ones[:], 1.0)
        warm = consts.tile([P, 1], F32)
        nc.scalar.activation(out=warm[:], in_=neg_half[:], func=ACT.Silu)
        ident_f32 = consts.tile([P, P], F32)
        make_identity(nc, ident_f32[:])
        ident_bf16 = consts.tile([P, P], BF16)
        make_identity(nc, ident_bf16[:])

        wo_raw = []
        for g in range(PASSES):
            raw = raw_pool.tile([P, PACK, LOAD_COLS], BF16, tag="raw")
            nc.sync.dma_start(
                out=raw[:].rearrange("q (u e) n -> q u e n", e=2),
                in_=w_o[g * K_PASS : (g + 1) * K_PASS, :].rearrange(
                    "(u q e) n -> q u e n", u=2, e=2
                ),
            )
            wo_raw.append(raw)
            if g == 0:
                nc.sync.dma_start(out=gain_row[0:1, :], in_=rms2_scale.unsqueeze(0))
        attn_sb = keep.tile([P, TOKEN_TILES, D_MODEL], BF16)
        for i in range(TOKEN_TILES):
            nc.sync.dma_start(out=attn_sb[:, i, :], in_=attn_rows[i * P : (i + 1) * P, :])
        x_sb = keep.tile([P, TOKEN_TILES, D_MODEL], BF16)
        for i in range(TOKEN_TILES):
            nc.sync.dma_start(out=x_sb[:, i, :], in_=x_rows[i * P : (i + 1) * P, :])
        for unit in range(RAW_BUFS):
            load_unit(unit)

        gain_banks = []
        for half in range(HALVES):
            gain_ps = banks.tile([P, N_TILE], F32, tag="bank")
            nc.tensor.matmul(
                out=gain_ps[:],
                lhsT=ones[:],
                rhs=gain_row[:, half * N_TILE : (half + 1) * N_TILE],
                start=True,
                stop=True,
            )
            gain_banks.append(gain_ps)

        wo_codes = keep.tile([P, PASSES, D_MODEL], U32, align_bytes=64)
        wo_scales = keep.tile([P, PASSES, D_MODEL], U8, align_bytes=64)
        by_vector = stage.tile([P, PASSES, N_TILE, PACK], BF16, align_bytes=64)
        by_scalar = stage.tile([P, PASSES, N_TILE, PACK], BF16, align_bytes=64)
        for g in range(PASSES):
            regroup(nc.vector.tensor_copy, by_vector[:, g], wo_raw[g][:, :, 0:N_TILE])
            regroup(nc.scalar.copy, by_scalar[:, g], wo_raw[g][:, :, N_TILE : 2 * N_TILE])
            for half, tile_ in enumerate((by_vector, by_scalar)):
                cols = slice(half * N_TILE, (half + 1) * N_TILE)
                nc.vector.quantize_mx(
                    out=wo_codes[:, g, cols].bitcast(FP8X4),
                    scales=wo_scales[:, g, cols],
                    in_=tile_[:, g].rearrange("p n t -> p (n t)"),
                )

        a_grouped = keep.tile([P, TOKEN_TILES, PASSES, P, PACK], BF16, align_bytes=64)
        a_codes = keep.tile([P, TOKEN_TILES, PASSES, P], U32, align_bytes=64)
        a_scales = keep.tile([P, TOKEN_TILES, PASSES, P], U8, align_bytes=64)
        for i in range(TOKEN_TILES):
            attn_words = attn_sb[:, i, :].bitcast(F32)
            at = banks.tile([P, PASSES, 2, P], F32, tag="bank")
            for g in range(PASSES):
                for u in range(2):
                    first = (2 * g + u) * P
                    nc.tensor.transpose(
                        out=at[:, g, u, :],
                        in_=attn_words[:, first : first + P],
                        identity=ident_f32[:],
                    )
            nc.scalar.copy(
                out=a_grouped[:, i].bitcast(F32),
                in_=at[:].rearrange("q g u r -> q g r u"),
            )
            nc.vector.quantize_mx(
                out=a_codes[:, i].rearrange("q g r -> q (g r)").bitcast(FP8X4),
                scales=a_scales[:, i].rearrange("q g r -> q (g r)"),
                in_=a_grouped[:, i].rearrange("q g r t -> q (g r t)"),
            )

        gain_all = consts.tile([P, D_MODEL], BF16)
        for half in range(HALVES):
            nc.scalar.mul(
                out=gain_all[:, half * N_TILE : (half + 1) * N_TILE],
                in_=gain_banks[half][:],
                mul=D_MODEL**0.5,
            )

        xmid = keep.tile([P, TOKEN_TILES, D_MODEL], F32)
        sumsq = keep.tile([P, TOKEN_TILES], F32)
        shifted = keep.tile([P, TOKEN_TILES], F32)
        inv_norm = keep.tile([P, TOKEN_TILES], F32)
        h_codes = keep.tile([P, TOKEN_TILES, PASSES, P], U32, align_bytes=64)
        h_scales = keep.tile([P, TOKEN_TILES, PASSES, P], U8, align_bytes=64)
        xm_banks = {}
        h_groups = {}

        def first_product(i):
            for half in range(HALVES):
                cols = slice(half * N_TILE, (half + 1) * N_TILE)
                xm_ps = banks.tile([P, N_TILE], F32, tag="bank")
                for g in range(PASSES):
                    nc.tensor.matmul_mx(
                        out=xm_ps[:],
                        lhsT=a_codes[:, i, g, :].bitcast(FP8X4),
                        lhsT_scale=a_scales[:, i, g, :],
                        rhs=wo_codes[:, g, cols].bitcast(FP8X4),
                        rhs_scale=wo_scales[:, g, cols],
                        start=(g == 0),
                        stop=(g == PASSES - 1),
                    )
                xm_banks[(i, half)] = xm_ps

        def add_and_square(i):
            one = slice(i, i + 1)
            for half in range(HALVES):
                cols = slice(half * N_TILE, (half + 1) * N_TILE)
                nc.vector.tensor_tensor(
                    out=xmid[:, i, cols], in0=xm_banks[(i, half)][:], in1=x_sb[:, i, cols], op=ALU.add
                )
            nc.sync.dma_start(out=xmid_rows[i * P : (i + 1) * P, :], in_=xmid[:, i, :])
            squares = rows.tile([P, D_MODEL], BF16)
            nc.scalar.activation(
                out=squares[:], in_=xmid[:, i, :], func=ACT.Square, accum_out=sumsq[:, one]
            )
            nc.gpsimd.tensor_scalar(
                out=shifted[:, one],
                in0=sumsq[:, one],
                scalar1=D_MODEL * EPS,
                scalar2=1.0,
                op0=ALU.add,
                op1=ALU.mult,
            )
            nc.gpsimd.tensor_tensor(
                out=inv_norm[:, one], in0=shifted[:, one], in1=neg_half[:], op=ALU.pow
            )

        def norm_and_transpose(i):
            h_bf16 = rows.tile([P, D_MODEL], BF16)
            nc.vector.scalar_tensor_tensor(
                out=h_bf16[:],
                in0=xmid[:, i, :],
                scalar=inv_norm[:, i : i + 1],
                in1=gain_all[:],
                op0=ALU.mult,
                op1=ALU.mult,
            )
            ht = banks.tile([P, PASSES * PACK, P], BF16, tag="bank")
            for j in range(PASSES * PACK):
                nc.tensor.transpose(
                    out=ht[:, j, :], in_=h_bf16[:, j * P : (j + 1) * P], identity=ident_bf16[:]
                )
            h_grouped = rows.tile([P, PASSES, P, PACK], BF16, align_bytes=64)
            nc.scalar.copy(out=h_grouped[:], in_=ht[:].rearrange("p (g t) r -> p g r t", t=PACK))
            h_groups[i] = h_grouped

        def quantise_h(i):
            nc.vector.quantize_mx(
                out=h_codes[:, i].rearrange("p g r -> p (g r)").bitcast(FP8X4),
                scales=h_scales[:, i].rearrange("p g r -> p (g r)"),
                in_=h_groups[i][:].rearrange("p g r t -> p (g r t)"),
            )

        for i in range(TOKEN_TILES):
            first_product(i)
            if i >= 1:
                add_and_square(i - 1)
        for i in range(TOKEN_TILES):
            norm_and_transpose(i)
            if i == 0:
                add_and_square(TOKEN_TILES - 1)
            vector_prepare(i)
            if i >= 1:
                quantise_h(i - 1)
                scalar_regroup(2 * i - 1)
            scalar_regroup(2 * i)
        vector_prepare(TOKEN_TILES)
        quantise_h(TOKEN_TILES - 1)
        for index in range(TOKEN_TILES + 1, LEAD):
            vector_prepare(index)

        for step in range(STEPS):
            chunk, i = divmod(step, TOKEN_TILES)
            gate_ps = banks.tile([P, N_TILE], F32, tag="bank")
            up_ps = banks.tile([P, N_TILE], F32, tag="bank")
            for m, product in enumerate((gate_ps, up_ps)):
                for g in range(PASSES):
                    nc.tensor.matmul_mx(
                        out=product[:],
                        lhsT=h_codes[:, i, g, :].bitcast(FP8X4),
                        lhsT_scale=h_scales[:, i, g, :],
                        rhs=w_codes[chunk][:, g, m, :].bitcast(FP8X4),
                        rhs_scale=w_scales[chunk][:, g, m, :],
                        start=(g == 0),
                        stop=(g == PASSES - 1),
                    )
            scalar_regroup(step + LEAD)
            silu = ep.tile([P, N_TILE], F32)
            nc.scalar.activation(out=silu[:], in_=gate_ps[:], func=ACT.Silu)
            vector_prepare(step + LEAD)
            g_sb = out_pool.tile([P, N_TILE], F32)
            nc.vector.tensor_tensor(out=g_sb[:], in0=up_ps[:], in1=silu[:], op=ALU.mult)
            first_col = chunk * N_TILE
            nc.sync.dma_start(
                out=g_rows[i * P : (i + 1) * P, first_col : first_col + N_TILE], in_=g_sb[:]
            )
